import numpy as np
import ml_dtypes


def mxq(x, axis, fmt="e4m3"):
    dtype, down = {"e4m3": (ml_dtypes.float8_e4m3fn, 7), "e5m2": (ml_dtypes.float8_e5m2, 14)}[fmt]
    v = np.moveaxis(np.asarray(x, np.float32).astype(ml_dtypes.bfloat16).astype(np.float64), axis, -1)
    blocks = v.reshape(v.shape[:-1] + (-1, 32))
    amax = np.abs(blocks).max(-1, keepdims=True)
    byte = np.maximum(np.where(amax > 0, np.frexp(amax)[1] - 1 + 127, 0) - down, 1)
    scale = np.exp2(byte - 127.0)
    codes = (blocks / scale).astype(np.float32).astype(dtype).astype(np.float64)
    return np.moveaxis((codes * scale).reshape(v.shape), -1, axis)


WIDE = False


def mx_kscale(k):
    if not WIDE:
        return np.ones(k)
    levels = np.array([10, -10, 5, -5, 0])
    a = np.random.permutation(np.resize(levels, k // 512 * 4)).reshape(k // 512, 4)
    idx = np.arange(k)
    return np.exp2(a[idx // 512, idx % 128 // 32])


BF16 = ml_dtypes.bfloat16


def bf(x):
    return np.asarray(x, np.float32).astype(BF16)


def f64(x):
    return np.asarray(x).astype(np.float64)


B, S, D, H, DN, DR, DV, RQ, RKV = 4, 1024, 512, 8, 64, 64, 128, 512, 512
THETA = 10000.0
EPS = 1e-6


def rmsnorm(v, w):
    return v * (1.0 / np.sqrt(np.mean(v * v, axis=-1, keepdims=True) + EPS)) * w


def rotate_half(v):
    v1 = v[..., ::2]
    v2 = v[..., 1::2]
    return np.stack((-v2, v1), axis=-1).reshape(v.shape)


def rope_cache():
    inv_freq = 1.0 / THETA ** (np.arange(0, DR, 2) / DR)
    freqs = np.outer(np.arange(S), inv_freq)
    emb = np.concatenate((freqs, freqs), -1)
    return np.cos(emb), np.sin(emb)


def apply_rope(v, cos, sin):
    return v * cos[None, None] + rotate_half(v) * sin[None, None]


def setup_inputs():
    s, t = mx_kscale(D), mx_kscale(RQ)
    return {"x": bf(np.random.standard_normal((B, S, D)) * s),
            "Wqa": bf(np.random.standard_normal((D, RQ)) / np.sqrt(D) / s[:, None]),
            "q_a_norm_w": bf((1.0 + 0.1 * np.random.standard_normal(RQ)) * t),
            "Wqb": bf(np.random.standard_normal((RQ, H * (DN + DR))) / np.sqrt(RQ) / t[:, None])}


def reference(x, Wqa, q_a_norm_w, Wqb):
    c = mxq(f64(x), 2, "e4m3") @ mxq(f64(Wqa), 0, "e4m3")
    h = rmsnorm(c, f64(q_a_norm_w))
    q = mxq(h, 2, "e4m3") @ mxq(f64(Wqb), 0, "e4m3")
    q = q.reshape(B, S, H, DN + DR).transpose(0, 2, 1, 3)
    q_nope, q_rope = q[..., :DN], q[..., DN:]
    cos, sin = rope_cache()
    q_rope = apply_rope(q_rope, cos, sin)
    return np.concatenate([q_nope, q_rope], -1)

@@ -1,0 +1,345 @@
+import math
+from contextlib import ExitStack
+
+import concourse.bass as bass
+import concourse.masks as masks
+import concourse.mybir as mybir
+import concourse.tile as tile
+
+F32 = mybir.dt.float32
+BF16 = mybir.dt.bfloat16
+I32 = mybir.dt.int32
+U32 = mybir.dt.uint32
+U8 = mybir.dt.uint8
+FP8X4 = mybir.dt.float8_e4m3fn_x4
+ALU = mybir.AluOpType
+ACT = mybir.ActivationFunctionType
+
+P = 128
+HEADS = 8
+N_UNITS = 8
+N_PAIRS = 16
+EPS = 1e-6
+FLOPS = 2 * 4096 * 512 * 512 + 2 * 4096 * 512 * 1024
+MANUAL = True
+
+
+def tile_multiheadlatentattention_pa_t_kernel(tc, x, Wqa, q_a_norm_w, Wqb, out):
+    nc = tc.nc
+    with ExitStack() as ctx:
+        if MANUAL:
+            ctx.enter_context(tc.manual_schedule())
+        const = ctx.enter_context(tc.tile_pool(name="const", bufs=1))
+        psum = ctx.enter_context(tc.psum_pool(name="psum", bufs=1))
+        work = ctx.enter_context(tc.tile_pool(name="work", bufs=3))
+        outp = ctx.enter_context(tc.tile_pool(name="outp", bufs=3))
+
+        x_units = x.flatten_outer_dims().rearrange("(u p i) d -> u p (i d)", u=N_UNITS, p=P, i=4)
+        wa_raw = const.tile([P, 4, 512], BF16, name="wa_raw")
+        nc.sync.dma_start(
+            out=wa_raw[:].rearrange("p (u e) c -> p u (e c)", u=2),
+            in_=Wqa.rearrange("(u q e) c -> q u (e c)", u=2, q=P, e=2),
+        )
+        x_sb = []
+        for u in range(N_UNITS):
+            x_sb.append(const.tile([P, 2048], BF16, name="x_sb%d" % u))
+        nc.sync.dma_start(out=x_sb[0][:, 0:1024], in_=x_units[0][:, 0:1024])
+        nc.sync.dma_start(out=x_sb[0][:, 1024:2048], in_=x_units[0][:, 1024:2048])
+        w_bc = const.tile([P, 512], BF16, name="w_bc")
+        nc.sync.dma_start(out=w_bc[:], in_=q_a_norm_w.partition_broadcast(P))
+        wb_raw = const.tile([P, 4, 1024], BF16, name="wb_raw")
+        nc.sync.dma_start(out=wb_raw[:], in_=Wqb.rearrange("(t p) n -> p t n", t=4, p=P))
+        for u in range(1, N_UNITS):
+            nc.sync.dma_start(out=x_sb[u][:], in_=x_units[u])
+
+        pos_i = const.tile([P, 8], I32, name="pos_i")
+        nc.gpsimd.iota(pos_i[:], pattern=[[512, 2], [1, 4]], base=0, channel_multiplier=4)
+        ident_f = const.tile([P, P], F32, name="ident_f")
+        masks.make_identity(nc, ident_f[:])
+        ident_b = const.tile([P, P], BF16, name="ident_b")
+        masks.make_identity(nc, ident_b[:])
+        eps_t = const.tile([P, 1], F32, name="eps_t")
+        nc.vector.memset(eps_t[:], EPS)
+
+        ratio = 10000.0 ** (-1.0 / 32.0)
+        turn = const.tile([P, 32], F32, name="turn")
+        one = const.tile([P, 1], F32, name="one")
+        nc.vector.memset(one[:], 1.0)
+        nc.vector.tensor_scalar_mul(out=turn[:, 0:1], in0=one[:], scalar1=1.0 / (2.0 * math.pi))
+        nc.vector.tensor_scalar_mul(out=turn[:, 1:2], in0=one[:], scalar1=ratio / (2.0 * math.pi))
+        for n in (2, 4, 8, 16):
+            nc.vector.tensor_scalar_mul(out=turn[:, n : 2 * n], in0=turn[:, 0:n], scalar1=ratio**n)
+        pos_f = const.tile([P, 8], F32, name="pos_f")
+        nc.vector.tensor_copy(out=pos_f[:], in_=pos_i[:])
+        turns = const.tile([P, 2, 8, 32], F32, name="turns")
+        nc.vector.tensor_tensor(
+            out=turns[:, 0],
+            in0=pos_f[:].unsqueeze(2).to_broadcast([P, 8, 32]),
+            in1=turn[:].unsqueeze(1).to_broadcast([P, 8, 32]),
+            op=ALU.mult,
+        )
+        nc.vector.tensor_scalar_add(out=turns[:, 1], in0=turns[:, 0], scalar1=0.25)
+        turns_flat = turns[:].rearrange("p s c f -> p (s c f)")
+        whole_i = const.tile([P, 512], I32, name="whole_i")
+        nc.vector.tensor_copy(out=whole_i[:], in_=turns_flat)
+        whole_f = const.tile([P, 512], F32, name="whole_f")
+        nc.vector.tensor_copy(out=whole_f[:], in_=whole_i[:])
+        frac = const.tile([P, 512], F32, name="frac")
+        nc.vector.tensor_tensor(out=frac[:], in0=turns_flat, in1=whole_f[:], op=ALU.subtract)
+        over = const.tile([P, 512], F32, name="over")
+        nc.vector.tensor_single_scalar(out=over[:], in_=frac[:], scalar=0.5, op=ALU.is_gt)
+        frac2 = const.tile([P, 512], F32, name="frac2")
+        nc.vector.tensor_tensor(out=frac2[:], in0=frac[:], in1=over[:], op=ALU.subtract)
+        sincos = const.tile([P, 2, 8, 32], F32, name="sincos")
+        nc.scalar.activation(
+            out=sincos[:].rearrange("p s c f -> p (s c f)"), in_=frac2[:], func=ACT.Sin, scale=2.0 * math.pi
+        )
+        warm = const.tile([P, 1], F32, name="warm")
+        nc.scalar.activation(out=warm[:], in_=eps_t[:], func=ACT.Sqrt)
+        ctab = const.tile([P, 8, 2, 32], F32, name="ctab")
+        stab = const.tile([P, 8, 2, 32], F32, name="stab")
+        for e in range(2):
+            for table, s, sign in ((ctab, 1, 1.0), (stab, 0, -1.0 if e == 0 else 1.0)):
+                src = sincos[:, s].rearrange("p c (j e) -> p c j e", e=2)[:, :, :, e]
+                nc.gpsimd.tensor_scalar(
+                    out=table[:, :, e, :].rearrange("p c (s j) -> p c s j", s=2),
+                    in0=src.unsqueeze(2).to_broadcast([P, 8, 2, 16]),
+                    scalar1=sign,
+                    scalar2=0.0,
+                    op0=ALU.mult,
+                    op1=ALU.add,
+                )
+
+        wa_grp = const.tile([P, 512, 4], BF16, name="wa_grp", align_bytes=64)
+        nc.vector.tensor_copy(
+            out=wa_grp[:].rearrange("p (c i) t -> p c t i", i=4),
+            in_=wa_raw[:].rearrange("p t (c i) -> p c t i", i=4),
+        )
+        wa_q = const.tile([P, 512], U32, name="wa_q", align_bytes=64)
+        wa_s = const.tile([P, 512], U8, name="wa_s", align_bytes=64)
+        nc.vector.quantize_mx(
+            out=wa_q[:].bitcast(FP8X4), scales=wa_s[:], in_=wa_grp[:].rearrange("p c t -> p (c t)")
+        )
+
+        wb_grp = const.tile([P, 1024, 4], BF16, name="wb_grp", align_bytes=64)
+        wb_q = const.tile([P, 1024], U32, name="wb_q", align_bytes=64)
+        wb_s = const.tile([P, 1024], U8, name="wb_s", align_bytes=64)
+
+        def wb_rope():
+            for e in range(2):
+                nc.vector.tensor_copy(
+                    out=wb_grp[:, 512:1024, :].rearrange("p (h e i) t -> p e h i t", h=HEADS, e=2)[:, e],
+                    in_=wb_raw[:].rearrange("p t (h z i e) -> p z e h i t", h=HEADS, z=2, e=2)[:, 1, e],
+                )
+            nc.vector.quantize_mx(
+                out=wb_q[:, 512:1024].bitcast(FP8X4),
+                scales=wb_s[:, 512:1024],
+                in_=wb_grp[:, 512:1024, :].rearrange("p c t -> p (c t)"),
+            )
+
+        def wb_nope():
+            nc.vector.tensor_copy(
+                out=wb_grp[:, 0:512, :].rearrange("p (h f) t -> p h f t", h=HEADS),
+                in_=wb_raw[:].rearrange("p t (h z f) -> p z h f t", h=HEADS, z=2)[:, 0],
+            )
+            nc.vector.quantize_mx(
+                out=wb_q[:, 0:512].bitcast(FP8X4),
+                scales=wb_s[:, 0:512],
+                in_=wb_grp[:, 0:512, :].rearrange("p c t -> p (c t)"),
+            )
+
+        st = {}
+
+        def tx(p):
+            xt = psum.tile([P, 2, 2, P], F32, name="xt", tag="xt")
+            st["xt", p] = xt
+            for a in range(2):
+                k = 2 * p + a
+                words = x_sb[k // 4][:].bitcast(F32)
+                for u in range(2):
+                    lo = (k % 4) * 256 + u * P
+                    nc.tensor.transpose(xt[:, a, u, :], words[:, lo : lo + P], ident_f[:])
+
+        def cx(p):
+            gx = work.tile([P, 1024], BF16, name="gx", tag="gx", align_bytes=64)
+            st["gx", p] = gx
+            nc.scalar.copy(
+                out=gx[:].bitcast(F32).rearrange("p (a r u) -> p a r u", a=2, u=2),
+                in_=st["xt", p][:].rearrange("p a u r -> p a r u"),
+            )
+
+        def qx(p):
+            xq = work.tile([P, 256], U32, name="xq", tag="xq", align_bytes=64)
+            xs = work.tile([P, 256], U8, name="xs", tag="xs", align_bytes=64)
+            st["xq", p] = (xq, xs)
+            nc.vector.quantize_mx(out=xq[:].bitcast(FP8X4), scales=xs[:], in_=st["gx", p][:])
+
+        def m1(p, a):
+            c = psum.tile([P, 512], F32, name="c%d" % a, tag="c%d" % a)
+            st["c", p, a] = c
+            xq, xs = st["xq", p]
+            nc.tensor.matmul_mx(
+                out=c[:],
+                lhsT=xq[:, a * P : (a + 1) * P].bitcast(FP8X4),
+                lhsT_scale=xs[:, a * P : (a + 1) * P],
+                rhs=wa_q[:].bitcast(FP8X4),
+                rhs_scale=wa_s[:],
+                start=True,
+                stop=True,
+            )
+
+        def sq(p, a):
+            if a == 0:
+                st["ssq", p] = work.tile([P, 2], F32, name="ssq", tag="ssq")
+            junk = work.tile([P, 512], BF16, name="junk", tag="junk")
+            nc.scalar.activation(
+                out=junk[:], in_=st["c", p, a][:], func=ACT.Square, accum_out=st["ssq", p][:, a : a + 1]
+            )
+
+        def sr(p):
+            rms = work.tile([P, 2], F32, name="rms", tag="rms")
+            st["rms", p] = rms
+            nc.scalar.activation(out=rms[:], in_=st["ssq", p][:], func=ACT.Sqrt, scale=1.0 / 512.0, bias=eps_t[:])
+
+        def rc(p):
+            rstd = work.tile([P, 2], F32, name="rstd", tag="rstd")
+            st["rstd", p] = rstd
+            nc.vector.reciprocal(out=rstd[:], in_=st["rms", p][:])
+
+        def hh(p, a):
+            h = work.tile([P, 512], BF16, name="h%d" % a, tag="h%d" % a)
+            st["h", p, a] = h
+            nc.vector.scalar_tensor_tensor(
+                out=h[:],
+                in0=st["c", p, a][:],
+                scalar=st["rstd", p][:, a : a + 1],
+                in1=w_bc[:],
+                op0=ALU.mult,
+                op1=ALU.mult,
+            )
+
+        def th(p):
+            ht = psum.tile([P, 2, 4, P], BF16, name="ht", tag="ht")
+            st["ht", p] = ht
+            for a in range(2):
+                for t in range(4):
+                    nc.tensor.transpose(ht[:, a, t, :], st["h", p, a][:, t * P : (t + 1) * P], ident_b[:])
+
+        def ch(p):
+            gh = work.tile([P, 1024], BF16, name="gh", tag="gh", align_bytes=64)
+            st["gh", p] = gh
+            nc.scalar.copy(
+                out=gh[:].rearrange("p (a r t) -> p a r t", a=2, t=4),
+                in_=st["ht", p][:].rearrange("p a t r -> p a r t"),
+            )
+
+        def qh(p):
+            hq = work.tile([P, 256], U32, name="hq", tag="hq", align_bytes=64)
+            hs = work.tile([P, 256], U8, name="hs", tag="hs", align_bytes=64)
+            st["hq", p] = (hq, hs)
+            nc.vector.quantize_mx(out=hq[:].bitcast(FP8X4), scales=hs[:], in_=st["gh", p][:])
+
+        def m2(p, a, z):
+            kind = "nr"[z]
+            acc = psum.tile([P, 512], F32, name="%s%d" % (kind, a), tag="%s%d" % (kind, a))
+            st[kind, p, a] = acc
+            hq, hs = st["hq", p]
+            nc.tensor.matmul_mx(
+                out=acc[:],
+                lhsT=hq[:, a * P : (a + 1) * P].bitcast(FP8X4),
+                lhsT_scale=hs[:, a * P : (a + 1) * P],
+                rhs=wb_q[:, z * 512 : (z + 1) * 512].bitcast(FP8X4),
+                rhs_scale=wb_s[:, z * 512 : (z + 1) * 512],
+                start=True,
+                stop=True,
+            )
+
+        def out_tile(u):
+            if ("o", u) not in st:
+                st["o", u] = outp.tile([P, HEADS, 4, P], F32, name="o_sb", tag="o_sb")
+            return st["o", u]
+
+        def cn(p, a):
+            k = 2 * p + a
+            nc.scalar.copy(
+                out=out_tile(k // 4)[:, :, k % 4, 0:64],
+                in_=st["n", p, a][:].rearrange("p (h f) -> p h f", h=HEADS),
+            )
+
+        def tt(p, a):
+            k = 2 * p + a
+            c = ((k // 4) % 2) * 4 + k % 4
+            r = st["r", p, a][:].rearrange("p (h e i) -> p h e i", h=HEADS, e=2)
+            t1 = work.tile([P, HEADS, 64], F32, name="t1", tag="t1")
+            t2 = work.tile([P, HEADS, 2, 32], F32, name="t2", tag="t2")
+            st["t", p, a] = (t1, t2)
+            nc.vector.tensor_tensor(
+                out=t1[:],
+                in0=st["r", p, a][:].rearrange("p (h f) -> p h f", h=HEADS),
+                in1=ctab[:, c].rearrange("p e i -> p (e i)").unsqueeze(1).to_broadcast([P, HEADS, 64]),
+                op=ALU.mult,
+            )
+            for e in range(2):
+                nc.vector.tensor_tensor(
+                    out=t2[:, :, e, :],
+                    in0=r[:, :, 1 - e, :],
+                    in1=stab[:, c, e, :].unsqueeze(1).to_broadcast([P, HEADS, 32]),
+                    op=ALU.mult,
+                )
+
+        def ad(p, a):
+            k = 2 * p + a
+            t1, t2 = st["t", p, a]
+            nc.gpsimd.tensor_tensor(
+                out=out_tile(k // 4)[:, :, k % 4, 64:128].rearrange("p h (i e) -> p h i e", e=2),
+                in0=t1[:].rearrange("p h (e i) -> p h i e", e=2),
+                in1=t2[:].rearrange("p h e i -> p h i e"),
+                op=ALU.add,
+            )
+
+        def store(p):
+            u = p // 2
+            dst = out[u // 2].rearrange("h (q p i) f -> q p h (i f)", q=2, p=P, i=4)[u % 2]
+            if u == N_UNITS - 1:
+                lo = (p % 2) * 2
+                nc.sync.dma_start(
+                    out=dst[:, :, lo * P : (lo + 2) * P],
+                    in_=st["o", u][:, :, lo : lo + 2, :].rearrange("p h i f -> p h (i f)"),
+                )
+            elif p % 2 == 1:
+                nc.sync.dma_start(out=dst, in_=st["o", u][:].rearrange("p h i f -> p h (i f)"))
+
+        def run(stage, p, *rest):
+            if 0 <= p < N_PAIRS:
+                stage(p, *rest)
+
+        for n in range(N_PAIRS + 6):
+            run(tx, n)
+            run(th, n - 3)
+            run(qh, n - 4)
+            run(sr, n - 2)
+            run(cx, n)
+            run(ad, n - 5, 0)
+            run(tt, n - 5, 1)
+            run(m2, n - 4, 0, 1)
+            run(cn, n - 5, 0)
+            run(cn, n - 5, 1)
+            run(rc, n - 2)
+            run(hh, n - 2, 0)
+            run(ad, n - 5, 1)
+            run(ch, n - 3)
+            run(store, n - 5)
+            run(hh, n - 2, 1)
+            if n == 2:
+                wb_rope()
+            if n == 3:
+                wb_nope()
+            run(m1, n - 1, 0)
+            run(m2, n - 4, 0, 0)
+            run(qx, n)
+            run(m1, n - 1, 1)
+            run(sq, n - 1, 0)
+            run(tt, n - 4, 0)
+            run(m2, n - 4, 1, 1)
+            run(m2, n - 4, 1, 0)
+            run(sq, n - 1, 1)

@@ -290,7 +290,8 @@ def tile_multiheadlatentattention_pa_t_kernel(tc, x, Wqa, q_a_norm_w, Wqb, out):
         def ad(p, a):
             k = 2 * p + a
             t1, t2 = st["t", p, a]
-            nc.gpsimd.tensor_tensor(
+            engine = nc.gpsimd if a == 0 else nc.vector
+            engine.tensor_tensor(
                 out=out_tile(k // 4)[:, :, k % 4, 64:128].rearrange("p h (i e) -> p h i e", e=2),
                 in0=t1[:].rearrange("p h (e i) -> p h i e", e=2),
                 in1=t2[:].rearrange("p h e i -> p h i e"),
@@ -326,10 +327,10 @@ def tile_multiheadlatentattention_pa_t_kernel(tc, x, Wqa, q_a_norm_w, Wqb, out):
             run(cn, n - 5, 1)
             run(rc, n - 2)
             run(hh, n - 2, 0)
-            run(ad, n - 5, 1)
             run(ch, n - 3)
-            run(store, n - 5)
             run(hh, n - 2, 1)
+            run(ad, n - 5, 1)
+            run(store, n - 5)
             if n == 2:
                 wb_rope()
             if n == 3:

@@ -21,14 +21,12 @@ N_UNITS = 8
 N_PAIRS = 16
 EPS = 1e-6
 FLOPS = 2 * 4096 * 512 * 512 + 2 * 4096 * 512 * 1024
-MANUAL = True
 
 
 def tile_multiheadlatentattention_pa_t_kernel(tc, x, Wqa, q_a_norm_w, Wqb, out):
     nc = tc.nc
     with ExitStack() as ctx:
-        if MANUAL:
-            ctx.enter_context(tc.manual_schedule())
+        ctx.enter_context(tc.manual_schedule())
         const = ctx.enter_context(tc.tile_pool(name="const", bufs=1))
         psum = ctx.enter_context(tc.psum_pool(name="psum", bufs=1))
         work = ctx.enter_context(tc.tile_pool(name="work", bufs=3))
@@ -45,11 +43,13 @@ def tile_multiheadlatentattention_pa_t_kernel(tc, x, Wqa, q_a_norm_w, Wqb, out):
             x_sb.append(const.tile([P, 2048], BF16, name="x_sb%d" % u))
         nc.sync.dma_start(out=x_sb[0][:, 0:1024], in_=x_units[0][:, 0:1024])
         nc.sync.dma_start(out=x_sb[0][:, 1024:2048], in_=x_units[0][:, 1024:2048])
+        nc.sync.dma_start(out=x_sb[1][:], in_=x_units[1])
         w_bc = const.tile([P, 512], BF16, name="w_bc")
         nc.sync.dma_start(out=w_bc[:], in_=q_a_norm_w.partition_broadcast(P))
+        nc.sync.dma_start(out=x_sb[2][:], in_=x_units[2])
         wb_raw = const.tile([P, 4, 1024], BF16, name="wb_raw")
         nc.sync.dma_start(out=wb_raw[:], in_=Wqb.rearrange("(t p) n -> p t n", t=4, p=P))
-        for u in range(1, N_UNITS):
+        for u in range(3, N_UNITS):
             nc.sync.dma_start(out=x_sb[u][:], in_=x_units[u])
 
         pos_i = const.tile([P, 8], I32, name="pos_i")
@@ -91,24 +91,27 @@ def tile_multiheadlatentattention_pa_t_kernel(tc, x, Wqa, q_a_norm_w, Wqb, out):
         frac2 = const.tile([P, 512], F32, name="frac2")
         nc.vector.tensor_tensor(out=frac2[:], in0=frac[:], in1=over[:], op=ALU.subtract)
         sincos = const.tile([P, 2, 8, 32], F32, name="sincos")
-        nc.scalar.activation(
-            out=sincos[:].rearrange("p s c f -> p (s c f)"), in_=frac2[:], func=ACT.Sin, scale=2.0 * math.pi
-        )
-        warm = const.tile([P, 1], F32, name="warm")
-        nc.scalar.activation(out=warm[:], in_=eps_t[:], func=ACT.Sqrt)
+        warm = const.tile([P, 2], F32, name="warm")
+        nc.scalar.activation(out=warm[:, 0:1], in_=one[:], func=ACT.Sin)
         ctab = const.tile([P, 8, 2, 32], F32, name="ctab")
         stab = const.tile([P, 8, 2, 32], F32, name="stab")
-        for e in range(2):
-            for table, s, sign in ((ctab, 1, 1.0), (stab, 0, -1.0 if e == 0 else 1.0)):
-                src = sincos[:, s].rearrange("p c (j e) -> p c j e", e=2)[:, :, :, e]
-                nc.gpsimd.tensor_scalar(
-                    out=table[:, :, e, :].rearrange("p c (s j) -> p c s j", s=2),
-                    in0=src.unsqueeze(2).to_broadcast([P, 8, 2, 16]),
-                    scalar1=sign,
-                    scalar2=0.0,
-                    op0=ALU.mult,
-                    op1=ALU.add,
-                )
+
+        def tables():
+            nc.scalar.activation(
+                out=sincos[:].rearrange("p s c f -> p (s c f)"), in_=frac2[:], func=ACT.Sin, scale=2.0 * math.pi
+            )
+            nc.scalar.activation(out=warm[:, 1:2], in_=eps_t[:], func=ACT.Sqrt)
+            for e in range(2):
+                for table, s, sign in ((ctab, 1, 1.0), (stab, 0, -1.0 if e == 0 else 1.0)):
+                    src = sincos[:, s].rearrange("p c (j e) -> p c j e", e=2)[:, :, :, e]
+                    nc.gpsimd.tensor_scalar(
+                        out=table[:, :, e, :].rearrange("p c (s j) -> p c s j", s=2),
+                        in0=src.unsqueeze(2).to_broadcast([P, 8, 2, 16]),
+                        scalar1=sign,
+                        scalar2=0.0,
+                        op0=ALU.mult,
+                        op1=ALU.add,
+                    )
 
         wa_grp = const.tile([P, 512, 4], BF16, name="wa_grp", align_bytes=64)
         nc.vector.tensor_copy(
@@ -148,10 +151,13 @@ def tile_multiheadlatentattention_pa_t_kernel(tc, x, Wqa, q_a_norm_w, Wqb, out):
                 in_=wb_grp[:, 0:512, :].rearrange("p c t -> p (c t)"),
             )
 
+        x_q = const.tile([P, N_PAIRS * 256], U32, name="x_q", align_bytes=64)
+        x_s = const.tile([P, N_PAIRS * 256], U8, name="x_s", align_bytes=64)
+
         st = {}
 
         def tx(p):
-            xt = psum.tile([P, 2, 2, P], F32, name="xt", tag="xt")
+            xt = psum.tile([P, 2, 2, P], F32, name="xt", tag=("r0", "n0", "r1", "n1")[p % 4])
             st["xt", p] = xt
             for a in range(2):
                 k = 2 * p + a
@@ -161,7 +167,7 @@ def tile_multiheadlatentattention_pa_t_kernel(tc, x, Wqa, q_a_norm_w, Wqb, out):
                     nc.tensor.transpose(xt[:, a, u, :], words[:, lo : lo + P], ident_f[:])
 
         def cx(p):
-            gx = work.tile([P, 1024], BF16, name="gx", tag="gx", align_bytes=64)
+            gx = work.tile([P, 1024], BF16, name="gx", tag="gx", bufs=4, align_bytes=64)
             st["gx", p] = gx
             nc.scalar.copy(
                 out=gx[:].bitcast(F32).rearrange("p (a r u) -> p a r u", a=2, u=2),
@@ -169,19 +175,17 @@ def tile_multiheadlatentattention_pa_t_kernel(tc, x, Wqa, q_a_norm_w, Wqb, out):
             )
 
         def qx(p):
-            xq = work.tile([P, 256], U32, name="xq", tag="xq", align_bytes=64)
-            xs = work.tile([P, 256], U8, name="xs", tag="xs", align_bytes=64)
-            st["xq", p] = (xq, xs)
-            nc.vector.quantize_mx(out=xq[:].bitcast(FP8X4), scales=xs[:], in_=st["gx", p][:])
+            cols = slice(p * 256, (p + 1) * 256)
+            nc.vector.quantize_mx(out=x_q[:, cols].bitcast(FP8X4), scales=x_s[:, cols], in_=st["gx", p][:])
 
         def m1(p, a):
-            c = psum.tile([P, 512], F32, name="c%d" % a, tag="c%d" % a)
+            k = 2 * p + a
+            c = psum.tile([P, 512], F32, name="c", tag="c%d" % (k % 3))
             st["c", p, a] = c
-            xq, xs = st["xq", p]
             nc.tensor.matmul_mx(
                 out=c[:],
-                lhsT=xq[:, a * P : (a + 1) * P].bitcast(FP8X4),
-                lhsT_scale=xs[:, a * P : (a + 1) * P],
+                lhsT=x_q[:, k * P : (k + 1) * P].bitcast(FP8X4),
+                lhsT_scale=x_s[:, k * P : (k + 1) * P],
                 rhs=wa_q[:].bitcast(FP8X4),
                 rhs_scale=wa_s[:],
                 start=True,
@@ -189,22 +193,22 @@ def tile_multiheadlatentattention_pa_t_kernel(tc, x, Wqa, q_a_norm_w, Wqb, out):
             )
 
         def sq(p, a):
-            if a == 0:
-                st["ssq", p] = work.tile([P, 2], F32, name="ssq", tag="ssq")
+            ssq = work.tile([P, 1], F32, name="ssq", tag="ssq%d" % a)
+            st["ssq", p, a] = ssq
             junk = work.tile([P, 512], BF16, name="junk", tag="junk")
+            nc.scalar.activation(out=junk[:], in_=st["c", p, a][:], func=ACT.Square, accum_out=ssq[:])
+
+        def sr(p, a):
+            rms = work.tile([P, 1], F32, name="rms", tag="rms%d" % a)
+            st["rms", p, a] = rms
             nc.scalar.activation(
-                out=junk[:], in_=st["c", p, a][:], func=ACT.Square, accum_out=st["ssq", p][:, a : a + 1]
+                out=rms[:], in_=st["ssq", p, a][:], func=ACT.Sqrt, scale=1.0 / 512.0, bias=eps_t[:]
             )
 
-        def sr(p):
-            rms = work.tile([P, 2], F32, name="rms", tag="rms")
-            st["rms", p] = rms
-            nc.scalar.activation(out=rms[:], in_=st["ssq", p][:], func=ACT.Sqrt, scale=1.0 / 512.0, bias=eps_t[:])
-
-        def rc(p):
-            rstd = work.tile([P, 2], F32, name="rstd", tag="rstd")
-            st["rstd", p] = rstd
-            nc.vector.reciprocal(out=rstd[:], in_=st["rms", p][:])
+        def rc(p, a):
+            rstd = work.tile([P, 1], F32, name="rstd", tag="rstd%d" % a)
+            st["rstd", p, a] = rstd
+            nc.vector.reciprocal(out=rstd[:], in_=st["rms", p, a][:])
 
         def hh(p, a):
             h = work.tile([P, 512], BF16, name="h%d" % a, tag="h%d" % a)
@@ -212,7 +216,7 @@ def tile_multiheadlatentattention_pa_t_kernel(tc, x, Wqa, q_a_norm_w, Wqb, out):
             nc.vector.scalar_tensor_tensor(
                 out=h[:],
                 in0=st["c", p, a][:],
-                scalar=st["rstd", p][:, a : a + 1],
+                scalar=st["rstd", p, a][:],
                 in1=w_bc[:],
                 op0=ALU.mult,
                 op1=ALU.mult,
@@ -290,7 +294,7 @@ def tile_multiheadlatentattention_pa_t_kernel(tc, x, Wqa, q_a_norm_w, Wqb, out):
         def ad(p, a):
             k = 2 * p + a
             t1, t2 = st["t", p, a]
-            engine = nc.gpsimd if a == 0 else nc.vector
+            engine = nc.vector if k == 2 * N_PAIRS - 1 else nc.gpsimd
             engine.tensor_tensor(
                 out=out_tile(k // 4)[:, :, k % 4, 64:128].rearrange("p h (i e) -> p h i e", e=2),
                 in0=t1[:].rearrange("p h (e i) -> p h i e", e=2),
@@ -298,49 +302,63 @@ def tile_multiheadlatentattention_pa_t_kernel(tc, x, Wqa, q_a_norm_w, Wqb, out):
                 op=ALU.add,
             )
 
-        def store(p):
-            u = p // 2
+        def store(u, lo, hi):
             dst = out[u // 2].rearrange("h (q p i) f -> q p h (i f)", q=2, p=P, i=4)[u % 2]
-            if u == N_UNITS - 1:
-                lo = (p % 2) * 2
-                nc.sync.dma_start(
-                    out=dst[:, :, lo * P : (lo + 2) * P],
-                    in_=st["o", u][:, :, lo : lo + 2, :].rearrange("p h i f -> p h (i f)"),
-                )
-            elif p % 2 == 1:
-                nc.sync.dma_start(out=dst, in_=st["o", u][:].rearrange("p h i f -> p h (i f)"))
+            nc.sync.dma_start(
+                out=dst[:, :, lo * P : hi * P],
+                in_=st["o", u][:, :, lo:hi, :].rearrange("p h i f -> p h (i f)"),
+            )
+
+        def done(p, a):
+            if p == N_PAIRS - 1:
+                store(N_UNITS - 1, 2 + a, 3 + a)
+            elif p == N_PAIRS - 2 and a == 1:
+                store(N_UNITS - 1, 0, 2)
+            elif p % 2 == 1 and a == 1:
+                store(p // 2, 0, 4)
 
         def run(stage, p, *rest):
             if 0 <= p < N_PAIRS:
                 stage(p, *rest)
 
-        for n in range(N_PAIRS + 6):
-            run(tx, n)
-            run(th, n - 3)
-            run(qh, n - 4)
-            run(sr, n - 2)
-            run(cx, n)
-            run(ad, n - 5, 0)
-            run(tt, n - 5, 1)
-            run(m2, n - 4, 0, 1)
-            run(cn, n - 5, 0)
-            run(cn, n - 5, 1)
-            run(rc, n - 2)
-            run(hh, n - 2, 0)
-            run(ch, n - 3)
-            run(hh, n - 2, 1)
-            run(ad, n - 5, 1)
-            run(store, n - 5)
-            if n == 2:
+        def x_stage(q):
+            run(tx, q)
+            run(cx, q - 2)
+            run(qx, q - 3)
+            if q == 4:
+                tables()
+
+        for n in range(-1, N_PAIRS + 4):
+            x_stage(4 * n + 4)
+            run(m1, n, 0)
+            run(m2, n - 3, 0, 1)
+            run(rc, n - 1, 1)
+            run(hh, n - 1, 1)
+            run(m1, n, 1)
+            run(tt, n - 3, 0)
+            x_stage(4 * n + 5)
+            run(ch, n - 2)
+            run(sq, n, 0)
+            run(ad, n - 4, 0)
+            run(done, n - 4, 0)
+            run(sr, n, 0)
+            run(sq, n, 1)
+            x_stage(4 * n + 6)
+            run(m2, n - 3, 0, 0)
+            run(m2, n - 3, 1, 1)
+            run(cn, n - 3, 0)
+            run(m2, n - 3, 1, 0)
+            run(qh, n - 2)
+            run(rc, n, 0)
+            run(th, n - 1)
+            run(sr, n, 1)
+            x_stage(4 * n + 7)
+            run(cn, n - 3, 1)
+            run(hh, n, 0)
+            run(ad, n - 4, 1)
+            run(done, n - 4, 1)
+            run(tt, n - 3, 1)
+            if n == 0:
                 wb_rope()
-            if n == 3:
+            if n == 1:
                 wb_nope()
-            run(m1, n - 1, 0)
-            run(m2, n - 4, 0, 0)
-            run(qx, n)
-            run(m1, n - 1, 1)
-            run(sq, n - 1, 0)
-            run(tt, n - 4, 0)
-            run(m2, n - 4, 1, 1)
-            run(m2, n - 4, 1, 0)
-            run(sq, n - 1, 1)

@@ -294,7 +294,7 @@ def tile_multiheadlatentattention_pa_t_kernel(tc, x, Wqa, q_a_norm_w, Wqb, out):
         def ad(p, a):
             k = 2 * p + a
             t1, t2 = st["t", p, a]
-            engine = nc.vector if k == 2 * N_PAIRS - 1 else nc.gpsimd
+            engine = nc.vector if k % 4 == 3 else nc.gpsimd
             engine.tensor_tensor(
                 out=out_tile(k // 4)[:, :, k % 4, 64:128].rearrange("p h (i e) -> p h i e", e=2),
                 in0=t1[:].rearrange("p h (e i) -> p h i e", e=2),

@@ -93,25 +93,33 @@ def tile_multiheadlatentattention_pa_t_kernel(tc, x, Wqa, q_a_norm_w, Wqb, out):
         sincos = const.tile([P, 2, 8, 32], F32, name="sincos")
         warm = const.tile([P, 2], F32, name="warm")
         nc.scalar.activation(out=warm[:, 0:1], in_=one[:], func=ACT.Sin)
-        ctab = const.tile([P, 8, 2, 32], F32, name="ctab")
-        stab = const.tile([P, 8, 2, 32], F32, name="stab")
+        tab = const.tile([P, 8, 2, 2, 32], F32, name="tab")
 
         def tables():
             nc.scalar.activation(
                 out=sincos[:].rearrange("p s c f -> p (s c f)"), in_=frac2[:], func=ACT.Sin, scale=2.0 * math.pi
             )
-            nc.scalar.activation(out=warm[:, 1:2], in_=eps_t[:], func=ACT.Sqrt)
+            nc.scalar.activation(out=warm[:, 1:2], in_=eps_t[:], func=ACT.Abs_reciprocal_sqrt)
+            nc.gpsimd.tensor_scalar(
+                out=tab[:, :, 0],
+                in0=sincos[:, 1].unsqueeze(2).to_broadcast([P, 8, 2, 32]),
+                scalar1=1.0,
+                scalar2=0.0,
+                op0=ALU.mult,
+                op1=ALU.add,
+            )
             for e in range(2):
-                for table, s, sign in ((ctab, 1, 1.0), (stab, 0, -1.0 if e == 0 else 1.0)):
-                    src = sincos[:, s].rearrange("p c (j e) -> p c j e", e=2)[:, :, :, e]
-                    nc.gpsimd.tensor_scalar(
-                        out=table[:, :, e, :].rearrange("p c (s j) -> p c s j", s=2),
-                        in0=src.unsqueeze(2).to_broadcast([P, 8, 2, 16]),
-                        scalar1=sign,
-                        scalar2=0.0,
-                        op0=ALU.mult,
-                        op1=ALU.add,
-                    )
+                nc.gpsimd.tensor_scalar(
+                    out=tab[:, :, 1].rearrange("p c s (j e) -> p c s j e", e=2)[:, :, :, :, e],
+                    in0=sincos[:, 0]
+                    .rearrange("p c (j e) -> p c j e", e=2)[:, :, :, 1 - e]
+                    .unsqueeze(2)
+                    .to_broadcast([P, 8, 2, 16]),
+                    scalar1=1.0 if e == 0 else -1.0,
+                    scalar2=0.0,
+                    op0=ALU.mult,
+                    op1=ALU.add,
+                )
 
         wa_grp = const.tile([P, 512, 4], BF16, name="wa_grp", align_bytes=64)
         nc.vector.tensor_copy(
@@ -129,11 +137,10 @@ def tile_multiheadlatentattention_pa_t_kernel(tc, x, Wqa, q_a_norm_w, Wqb, out):
         wb_s = const.tile([P, 1024], U8, name="wb_s", align_bytes=64)
 
         def wb_rope():
-            for e in range(2):
-                nc.vector.tensor_copy(
-                    out=wb_grp[:, 512:1024, :].rearrange("p (h e i) t -> p e h i t", h=HEADS, e=2)[:, e],
-                    in_=wb_raw[:].rearrange("p t (h z i e) -> p z e h i t", h=HEADS, z=2, e=2)[:, 1, e],
-                )
+            nc.scalar.copy(
+                out=wb_grp[:, 512:1024, :].rearrange("p (h f) t -> p h f t", h=HEADS),
+                in_=wb_raw[:].rearrange("p t (h z f) -> p z h f t", h=HEADS, z=2)[:, 1],
+            )
             nc.vector.quantize_mx(
                 out=wb_q[:, 512:1024].bitcast(FP8X4),
                 scales=wb_s[:, 512:1024],
@@ -141,7 +148,7 @@ def tile_multiheadlatentattention_pa_t_kernel(tc, x, Wqa, q_a_norm_w, Wqb, out):
             )
 
         def wb_nope():
-            nc.vector.tensor_copy(
+            nc.scalar.copy(
                 out=wb_grp[:, 0:512, :].rearrange("p (h f) t -> p h f t", h=HEADS),
                 in_=wb_raw[:].rearrange("p t (h z f) -> p z h f t", h=HEADS, z=2)[:, 0],
             )
@@ -199,16 +206,15 @@ def tile_multiheadlatentattention_pa_t_kernel(tc, x, Wqa, q_a_norm_w, Wqb, out):
             nc.scalar.activation(out=junk[:], in_=st["c", p, a][:], func=ACT.Square, accum_out=ssq[:])
 
         def sr(p, a):
-            rms = work.tile([P, 1], F32, name="rms", tag="rms%d" % a)
-            st["rms", p, a] = rms
-            nc.scalar.activation(
-                out=rms[:], in_=st["ssq", p, a][:], func=ACT.Sqrt, scale=1.0 / 512.0, bias=eps_t[:]
-            )
-
-        def rc(p, a):
             rstd = work.tile([P, 1], F32, name="rstd", tag="rstd%d" % a)
             st["rstd", p, a] = rstd
-            nc.vector.reciprocal(out=rstd[:], in_=st["rms", p, a][:])
+            nc.scalar.activation(
+                out=rstd[:],
+                in_=st["ssq", p, a][:],
+                func=ACT.Abs_reciprocal_sqrt,
+                scale=1.0 / 512.0,
+                bias=eps_t[:],
+            )
 
         def hh(p, a):
             h = work.tile([P, 512], BF16, name="h%d" % a, tag="h%d" % a)
@@ -273,32 +279,23 @@ def tile_multiheadlatentattention_pa_t_kernel(tc, x, Wqa, q_a_norm_w, Wqb, out):
         def tt(p, a):
             k = 2 * p + a
             c = ((k // 4) % 2) * 4 + k % 4
-            r = st["r", p, a][:].rearrange("p (h e i) -> p h e i", h=HEADS, e=2)
-            t1 = work.tile([P, HEADS, 64], F32, name="t1", tag="t1")
-            t2 = work.tile([P, HEADS, 2, 32], F32, name="t2", tag="t2")
-            st["t", p, a] = (t1, t2)
+            prod = work.tile([P, 2, HEADS, 64], F32, name="prod", tag="prod")
+            st["t", p, a] = prod
             nc.vector.tensor_tensor(
-                out=t1[:],
-                in0=st["r", p, a][:].rearrange("p (h f) -> p h f", h=HEADS),
-                in1=ctab[:, c].rearrange("p e i -> p (e i)").unsqueeze(1).to_broadcast([P, HEADS, 64]),
+                out=prod[:],
+                in0=st["r", p, a][:].rearrange("p (h f) -> p h f", h=HEADS).unsqueeze(1).to_broadcast([P, 2, HEADS, 64]),
+                in1=tab[:, c].rearrange("p z s f -> p z (s f)").unsqueeze(2).to_broadcast([P, 2, HEADS, 64]),
                 op=ALU.mult,
             )
-            for e in range(2):
-                nc.vector.tensor_tensor(
-                    out=t2[:, :, e, :],
-                    in0=r[:, :, 1 - e, :],
-                    in1=stab[:, c, e, :].unsqueeze(1).to_broadcast([P, HEADS, 32]),
-                    op=ALU.mult,
-                )
 
         def ad(p, a):
             k = 2 * p + a
-            t1, t2 = st["t", p, a]
-            engine = nc.vector if k % 4 == 3 else nc.gpsimd
+            prod = st["t", p, a]
+            engine = nc.vector if k == 2 * N_PAIRS - 1 else nc.gpsimd
             engine.tensor_tensor(
                 out=out_tile(k // 4)[:, :, k % 4, 64:128].rearrange("p h (i e) -> p h i e", e=2),
-                in0=t1[:].rearrange("p h (e i) -> p h i e", e=2),
-                in1=t2[:].rearrange("p h e i -> p h i e"),
+                in0=prod[:, 0].rearrange("p h (i e) -> p h i e", e=2),
+                in1=prod[:, 1].rearrange("p h (i e) -> p h i e", e=2)[:, :, :, ::-1],
                 op=ALU.add,
             )
 
@@ -332,7 +329,6 @@ def tile_multiheadlatentattention_pa_t_kernel(tc, x, Wqa, q_a_norm_w, Wqb, out):
             x_stage(4 * n + 4)
             run(m1, n, 0)
             run(m2, n - 3, 0, 1)
-            run(rc, n - 1, 1)
             run(hh, n - 1, 1)
             run(m1, n, 1)
             run(tt, n - 3, 0)
@@ -349,7 +345,6 @@ def tile_multiheadlatentattention_pa_t_kernel(tc, x, Wqa, q_a_norm_w, Wqb, out):
             run(cn, n - 3, 0)
             run(m2, n - 3, 1, 0)
             run(qh, n - 2)
-            run(rc, n, 0)
             run(th, n - 1)
             run(sr, n, 1)
             x_stage(4 * n + 7)

@@ -137,7 +137,7 @@ def tile_multiheadlatentattention_pa_t_kernel(tc, x, Wqa, q_a_norm_w, Wqb, out):
         wb_s = const.tile([P, 1024], U8, name="wb_s", align_bytes=64)
 
         def wb_rope():
-            nc.scalar.copy(
+            nc.vector.tensor_copy(
                 out=wb_grp[:, 512:1024, :].rearrange("p (h f) t -> p h f t", h=HEADS),
                 in_=wb_raw[:].rearrange("p t (h z f) -> p z h f t", h=HEADS, z=2)[:, 1],
             )
@@ -148,7 +148,7 @@ def tile_multiheadlatentattention_pa_t_kernel(tc, x, Wqa, q_a_norm_w, Wqb, out):
             )
 
         def wb_nope():
-            nc.scalar.copy(
+            nc.vector.tensor_copy(
                 out=wb_grp[:, 0:512, :].rearrange("p (h f) t -> p h f t", h=HEADS),
                 in_=wb_raw[:].rearrange("p t (h z f) -> p z h f t", h=HEADS, z=2)[:, 0],
             )
@@ -176,10 +176,12 @@ def tile_multiheadlatentattention_pa_t_kernel(tc, x, Wqa, q_a_norm_w, Wqb, out):
         def cx(p):
             gx = work.tile([P, 1024], BF16, name="gx", tag="gx", bufs=4, align_bytes=64)
             st["gx", p] = gx
-            nc.scalar.copy(
-                out=gx[:].bitcast(F32).rearrange("p (a r u) -> p a r u", a=2, u=2),
-                in_=st["xt", p][:].rearrange("p a u r -> p a r u"),
-            )
+            dst = gx[:].bitcast(F32).rearrange("p (a r u) -> p a r u", a=2, u=2)
+            src = st["xt", p][:].rearrange("p a u r -> p a r u")
+            if p % 4 == 3:
+                nc.vector.tensor_copy(out=dst, in_=src)
+            else:
+                nc.scalar.copy(out=dst, in_=src)
 
         def qx(p):
             cols = slice(p * 256, (p + 1) * 256)
@@ -291,7 +293,7 @@ def tile_multiheadlatentattention_pa_t_kernel(tc, x, Wqa, q_a_norm_w, Wqb, out):
         def ad(p, a):
             k = 2 * p + a
             prod = st["t", p, a]
-            engine = nc.vector if k == 2 * N_PAIRS - 1 else nc.gpsimd
+            engine = nc.vector if k // 4 == N_UNITS - 1 else nc.gpsimd
             engine.tensor_tensor(
                 out=out_tile(k // 4)[:, :, k % 4, 64:128].rearrange("p h (i e) -> p h i e", e=2),
                 in0=prod[:, 0].rearrange("p h (i e) -> p h i e", e=2),
@@ -337,8 +339,8 @@ def tile_multiheadlatentattention_pa_t_kernel(tc, x, Wqa, q_a_norm_w, Wqb, out):
             run(sq, n, 0)
             run(ad, n - 4, 0)
             run(done, n - 4, 0)
-            run(sr, n, 0)
             run(sq, n, 1)
+            run(sr, n, 0)
             x_stage(4 * n + 6)
             run(m2, n - 3, 0, 0)
             run(m2, n - 3, 1, 1)

@@ -178,10 +178,7 @@ def tile_multiheadlatentattention_pa_t_kernel(tc, x, Wqa, q_a_norm_w, Wqb, out):
             st["gx", p] = gx
             dst = gx[:].bitcast(F32).rearrange("p (a r u) -> p a r u", a=2, u=2)
             src = st["xt", p][:].rearrange("p a u r -> p a r u")
-            if p % 4 == 3:
-                nc.vector.tensor_copy(out=dst, in_=src)
-            else:
-                nc.scalar.copy(out=dst, in_=src)
+            nc.scalar.copy(out=dst, in_=src)
 
         def qx(p):
             cols = slice(p * 256, (p + 1) * 256)
@@ -235,7 +232,9 @@ def tile_multiheadlatentattention_pa_t_kernel(tc, x, Wqa, q_a_norm_w, Wqb, out):
             st["ht", p] = ht
             for a in range(2):
                 for t in range(4):
-                    nc.tensor.transpose(ht[:, a, t, :], st["h", p, a][:, t * P : (t + 1) * P], ident_b[:])
+                    nc.tensor.matmul(
+                        out=ht[:, a, t, :], lhsT=st["h", p, a][:, t * P : (t + 1) * P], rhs=ident_b[:], start=True, stop=True
+                    )
 
         def ch(p):
             gh = work.tile([P, 1024], BF16, name="gh", tag="gh", align_bytes=64)

@@ -43,13 +43,14 @@ def tile_multiheadlatentattention_pa_t_kernel(tc, x, Wqa, q_a_norm_w, Wqb, out):
             x_sb.append(const.tile([P, 2048], BF16, name="x_sb%d" % u))
         nc.sync.dma_start(out=x_sb[0][:, 0:1024], in_=x_units[0][:, 0:1024])
         nc.sync.dma_start(out=x_sb[0][:, 1024:2048], in_=x_units[0][:, 1024:2048])
-        nc.sync.dma_start(out=x_sb[1][:], in_=x_units[1])
-        w_bc = const.tile([P, 512], BF16, name="w_bc")
-        nc.sync.dma_start(out=w_bc[:], in_=q_a_norm_w.partition_broadcast(P))
-        nc.sync.dma_start(out=x_sb[2][:], in_=x_units[2])
+        w_row = const.tile([P, 512], BF16, name="w_row")
+        nc.gpsimd.memset(w_row[:], 0.0)
+        nc.sync.dma_start(out=w_row[0:1, :], in_=q_a_norm_w.rearrange("(o r) -> o r", o=1))
+        for u in range(1, 4):
+            nc.sync.dma_start(out=x_sb[u][:], in_=x_units[u])
         wb_raw = const.tile([P, 4, 1024], BF16, name="wb_raw")
         nc.sync.dma_start(out=wb_raw[:], in_=Wqb.rearrange("(t p) n -> p t n", t=4, p=P))
-        for u in range(3, N_UNITS):
+        for u in range(4, N_UNITS):
             nc.sync.dma_start(out=x_sb[u][:], in_=x_units[u])
 
         pos_i = const.tile([P, 8], I32, name="pos_i")
@@ -60,6 +61,14 @@ def tile_multiheadlatentattention_pa_t_kernel(tc, x, Wqa, q_a_norm_w, Wqb, out):
         masks.make_identity(nc, ident_b[:])
         eps_t = const.tile([P, 1], F32, name="eps_t")
         nc.vector.memset(eps_t[:], EPS)
+        ones_b = const.tile([P, P], BF16, name="ones_b")
+        nc.gpsimd.memset(ones_b[:], 1.0)
+        w_bc = const.tile([P, 512], BF16, name="w_bc")
+
+        def spread_gain():
+            w_ps = psum.tile([P, 512], F32, name="w_ps", tag="ht")
+            nc.tensor.matmul(out=w_ps[:], lhsT=ones_b[:], rhs=w_row[:], start=True, stop=True)
+            nc.vector.tensor_copy(out=w_bc[:], in_=w_ps[:])
 
         ratio = 10000.0 ** (-1.0 / 32.0)
         turn = const.tile([P, 32], F32, name="turn")
@@ -86,10 +95,6 @@ def tile_multiheadlatentattention_pa_t_kernel(tc, x, Wqa, q_a_norm_w, Wqb, out):
         nc.vector.tensor_copy(out=whole_f[:], in_=whole_i[:])
         frac = const.tile([P, 512], F32, name="frac")
         nc.vector.tensor_tensor(out=frac[:], in0=turns_flat, in1=whole_f[:], op=ALU.subtract)
-        over = const.tile([P, 512], F32, name="over")
-        nc.vector.tensor_single_scalar(out=over[:], in_=frac[:], scalar=0.5, op=ALU.is_gt)
-        frac2 = const.tile([P, 512], F32, name="frac2")
-        nc.vector.tensor_tensor(out=frac2[:], in0=frac[:], in1=over[:], op=ALU.subtract)
         sincos = const.tile([P, 2, 8, 32], F32, name="sincos")
         warm = const.tile([P, 2], F32, name="warm")
         nc.scalar.activation(out=warm[:, 0:1], in_=one[:], func=ACT.Sin)
@@ -97,7 +102,7 @@ def tile_multiheadlatentattention_pa_t_kernel(tc, x, Wqa, q_a_norm_w, Wqb, out):
 
         def tables():
             nc.scalar.activation(
-                out=sincos[:].rearrange("p s c f -> p (s c f)"), in_=frac2[:], func=ACT.Sin, scale=2.0 * math.pi
+                out=sincos[:].rearrange("p s c f -> p (s c f)"), in_=frac[:], func=ACT.Sin, scale=2.0 * math.pi
             )
             nc.scalar.activation(out=warm[:, 1:2], in_=eps_t[:], func=ACT.Abs_reciprocal_sqrt)
             nc.gpsimd.tensor_scalar(
@@ -292,7 +297,7 @@ def tile_multiheadlatentattention_pa_t_kernel(tc, x, Wqa, q_a_norm_w, Wqb, out):
         def ad(p, a):
             k = 2 * p + a
             prod = st["t", p, a]
-            engine = nc.vector if k // 4 == N_UNITS - 1 else nc.gpsimd
+            engine = nc.vector if p == N_PAIRS - 1 else nc.gpsimd
             engine.tensor_tensor(
                 out=out_tile(k // 4)[:, :, k % 4, 64:128].rearrange("p h (i e) -> p h i e", e=2),
                 in0=prod[:, 0].rearrange("p h (i e) -> p h i e", e=2),
@@ -323,9 +328,10 @@ def tile_multiheadlatentattention_pa_t_kernel(tc, x, Wqa, q_a_norm_w, Wqb, out):
             run(tx, q)
             run(cx, q - 2)
             run(qx, q - 3)
-            if q == 4:
-                tables()
+            if q == 3:
+                spread_gain()
 
+        tables()
         for n in range(-1, N_PAIRS + 4):
             x_stage(4 * n + 4)
             run(m1, n, 0)

import math
from contextlib import ExitStack

import concourse.bass as bass
import concourse.masks as masks
import concourse.mybir as mybir
import concourse.tile as tile

F32 = mybir.dt.float32
BF16 = mybir.dt.bfloat16
I32 = mybir.dt.int32
U32 = mybir.dt.uint32
U8 = mybir.dt.uint8
FP8X4 = mybir.dt.float8_e4m3fn_x4
ALU = mybir.AluOpType
ACT = mybir.ActivationFunctionType

P = 128
HEADS = 8
N_UNITS = 8
N_PAIRS = 16
EPS = 1e-6
FLOPS = 2 * 4096 * 512 * 512 + 2 * 4096 * 512 * 1024


def tile_multiheadlatentattention_pa_t_kernel(tc, x, Wqa, q_a_norm_w, Wqb, out):
    nc = tc.nc
    with ExitStack() as ctx:
        ctx.enter_context(tc.manual_schedule())
        const = ctx.enter_context(tc.tile_pool(name="const", bufs=1))
        psum = ctx.enter_context(tc.psum_pool(name="psum", bufs=1))
        work = ctx.enter_context(tc.tile_pool(name="work", bufs=3))
        outp = ctx.enter_context(tc.tile_pool(name="outp", bufs=3))

        x_units = x.flatten_outer_dims().rearrange("(u p i) d -> u p (i d)", u=N_UNITS, p=P, i=4)
        wa_raw = const.tile([P, 4, 512], BF16, name="wa_raw")
        nc.sync.dma_start(
            out=wa_raw[:].rearrange("p (u e) c -> p u (e c)", u=2),
            in_=Wqa.rearrange("(u q e) c -> q u (e c)", u=2, q=P, e=2),
        )
        x_sb = []
        for u in range(N_UNITS):
            x_sb.append(const.tile([P, 2048], BF16, name="x_sb%d" % u))
        nc.sync.dma_start(out=x_sb[0][:, 0:1024], in_=x_units[0][:, 0:1024])
        nc.sync.dma_start(out=x_sb[0][:, 1024:2048], in_=x_units[0][:, 1024:2048])
        w_row = const.tile([P, 512], BF16, name="w_row")
        nc.gpsimd.memset(w_row[:], 0.0)
        nc.sync.dma_start(out=w_row[0:1, :], in_=q_a_norm_w.rearrange("(o r) -> o r", o=1))
        for u in range(1, 4):
            nc.sync.dma_start(out=x_sb[u][:], in_=x_units[u])
        wb_raw = const.tile([P, 4, 1024], BF16, name="wb_raw")
        nc.sync.dma_start(out=wb_raw[:], in_=Wqb.rearrange("(t p) n -> p t n", t=4, p=P))
        for u in range(4, N_UNITS):
            nc.sync.dma_start(out=x_sb[u][:], in_=x_units[u])

        pos_i = const.tile([P, 8], I32, name="pos_i")
        nc.gpsimd.iota(pos_i[:], pattern=[[512, 2], [1, 4]], base=0, channel_multiplier=4)
        ident_f = const.tile([P, P], F32, name="ident_f")
        masks.make_identity(nc, ident_f[:])
        ident_b = const.tile([P, P], BF16, name="ident_b")
        masks.make_identity(nc, ident_b[:])
        eps_t = const.tile([P, 1], F32, name="eps_t")
        nc.vector.memset(eps_t[:], EPS)
        ones_b = const.tile([P, P], BF16, name="ones_b")
        nc.gpsimd.memset(ones_b[:], 1.0)
        w_bc = const.tile([P, 512], BF16, name="w_bc")

        def spread_gain():
            w_ps = psum.tile([P, 512], F32, name="w_ps", tag="ht")
            nc.tensor.matmul(out=w_ps[:], lhsT=ones_b[:], rhs=w_row[:], start=True, stop=True)
            nc.vector.tensor_copy(out=w_bc[:], in_=w_ps[:])

        ratio = 10000.0 ** (-1.0 / 32.0)
        turn = const.tile([P, 32], F32, name="turn")
        one = const.tile([P, 1], F32, name="one")
        nc.vector.memset(one[:], 1.0)
        nc.vector.tensor_scalar_mul(out=turn[:, 0:1], in0=one[:], scalar1=1.0 / (2.0 * math.pi))
        nc.vector.tensor_scalar_mul(out=turn[:, 1:2], in0=one[:], scalar1=ratio / (2.0 * math.pi))
        for n in (2, 4, 8, 16):
            nc.vector.tensor_scalar_mul(out=turn[:, n : 2 * n], in0=turn[:, 0:n], scalar1=ratio**n)
        pos_f = const.tile([P, 8], F32, name="pos_f")
        nc.vector.tensor_copy(out=pos_f[:], in_=pos_i[:])
        turns = const.tile([P, 2, 8, 32], F32, name="turns")
        nc.vector.tensor_tensor(
            out=turns[:, 0],
            in0=pos_f[:].unsqueeze(2).to_broadcast([P, 8, 32]),
            in1=turn[:].unsqueeze(1).to_broadcast([P, 8, 32]),
            op=ALU.mult,
        )
        nc.vector.tensor_scalar_add(out=turns[:, 1], in0=turns[:, 0], scalar1=0.25)
        turns_flat = turns[:].rearrange("p s c f -> p (s c f)")
        whole_i = const.tile([P, 512], I32, name="whole_i")
        nc.vector.tensor_copy(out=whole_i[:], in_=turns_flat)
        whole_f = const.tile([P, 512], F32, name="whole_f")
        nc.vector.tensor_copy(out=whole_f[:], in_=whole_i[:])
        frac = const.tile([P, 512], F32, name="frac")
        nc.vector.tensor_tensor(out=frac[:], in0=turns_flat, in1=whole_f[:], op=ALU.subtract)
        sincos = const.tile([P, 2, 8, 32], F32, name="sincos")
        warm = const.tile([P, 2], F32, name="warm")
        nc.scalar.activation(out=warm[:, 0:1], in_=one[:], func=ACT.Sin)
        tab = const.tile([P, 8, 2, 2, 32], F32, name="tab")

        def tables():
            nc.scalar.activation(
                out=sincos[:].rearrange("p s c f -> p (s c f)"), in_=frac[:], func=ACT.Sin, scale=2.0 * math.pi
            )
            nc.scalar.activation(out=warm[:, 1:2], in_=eps_t[:], func=ACT.Abs_reciprocal_sqrt)
            nc.gpsimd.tensor_scalar(
                out=tab[:, :, 0],
                in0=sincos[:, 1].unsqueeze(2).to_broadcast([P, 8, 2, 32]),
                scalar1=1.0,
                scalar2=0.0,
                op0=ALU.mult,
                op1=ALU.add,
            )
            for e in range(2):
                nc.gpsimd.tensor_scalar(
                    out=tab[:, :, 1].rearrange("p c s (j e) -> p c s j e", e=2)[:, :, :, :, e],
                    in0=sincos[:, 0]
                    .rearrange("p c (j e) -> p c j e", e=2)[:, :, :, 1 - e]
                    .unsqueeze(2)
                    .to_broadcast([P, 8, 2, 16]),
                    scalar1=1.0 if e == 0 else -1.0,
                    scalar2=0.0,
                    op0=ALU.mult,
                    op1=ALU.add,
                )

        wa_grp = const.tile([P, 512, 4], BF16, name="wa_grp", align_bytes=64)
        nc.vector.tensor_copy(
            out=wa_grp[:].rearrange("p (c i) t -> p c t i", i=4),
            in_=wa_raw[:].rearrange("p t (c i) -> p c t i", i=4),
        )
        wa_q = const.tile([P, 512], U32, name="wa_q", align_bytes=64)
        wa_s = const.tile([P, 512], U8, name="wa_s", align_bytes=64)
        nc.vector.quantize_mx(
            out=wa_q[:].bitcast(FP8X4), scales=wa_s[:], in_=wa_grp[:].rearrange("p c t -> p (c t)")
        )

        wb_grp = const.tile([P, 1024, 4], BF16, name="wb_grp", align_bytes=64)
        wb_q = const.tile([P, 1024], U32, name="wb_q", align_bytes=64)
        wb_s = const.tile([P, 1024], U8, name="wb_s", align_bytes=64)

        def wb_rope():
            nc.vector.tensor_copy(
                out=wb_grp[:, 512:1024, :].rearrange("p (h f) t -> p h f t", h=HEADS),
                in_=wb_raw[:].rearrange("p t (h z f) -> p z h f t", h=HEADS, z=2)[:, 1],
            )
            nc.vector.quantize_mx(
                out=wb_q[:, 512:1024].bitcast(FP8X4),
                scales=wb_s[:, 512:1024],
                in_=wb_grp[:, 512:1024, :].rearrange("p c t -> p (c t)"),
            )

        def wb_nope():
            nc.vector.tensor_copy(
                out=wb_grp[:, 0:512, :].rearrange("p (h f) t -> p h f t", h=HEADS),
                in_=wb_raw[:].rearrange("p t (h z f) -> p z h f t", h=HEADS, z=2)[:, 0],
            )
            nc.vector.quantize_mx(
                out=wb_q[:, 0:512].bitcast(FP8X4),
                scales=wb_s[:, 0:512],
                in_=wb_grp[:, 0:512, :].rearrange("p c t -> p (c t)"),
            )

        x_q = const.tile([P, N_PAIRS * 256], U32, name="x_q", align_bytes=64)
        x_s = const.tile([P, N_PAIRS * 256], U8, name="x_s", align_bytes=64)

        st = {}

        def tx(p):
            xt = psum.tile([P, 2, 2, P], F32, name="xt", tag=("r0", "n0", "r1", "n1")[p % 4])
            st["xt", p] = xt
            for a in range(2):
                k = 2 * p + a
                words = x_sb[k // 4][:].bitcast(F32)
                for u in range(2):
                    lo = (k % 4) * 256 + u * P
                    nc.tensor.transpose(xt[:, a, u, :], words[:, lo : lo + P], ident_f[:])

        def cx(p):
            gx = work.tile([P, 1024], BF16, name="gx", tag="gx", bufs=4, align_bytes=64)
            st["gx", p] = gx
            dst = gx[:].bitcast(F32).rearrange("p (a r u) -> p a r u", a=2, u=2)
            src = st["xt", p][:].rearrange("p a u r -> p a r u")
            nc.scalar.copy(out=dst, in_=src)

        def qx(p):
            cols = slice(p * 256, (p + 1) * 256)
            nc.vector.quantize_mx(out=x_q[:, cols].bitcast(FP8X4), scales=x_s[:, cols], in_=st["gx", p][:])

        def m1(p, a):
            k = 2 * p + a
            c = psum.tile([P, 512], F32, name="c", tag="c%d" % (k % 3))
            st["c", p, a] = c
            nc.tensor.matmul_mx(
                out=c[:],
                lhsT=x_q[:, k * P : (k + 1) * P].bitcast(FP8X4),
                lhsT_scale=x_s[:, k * P : (k + 1) * P],
                rhs=wa_q[:].bitcast(FP8X4),
                rhs_scale=wa_s[:],
                start=True,
                stop=True,
            )

        def sq(p, a):
            ssq = work.tile([P, 1], F32, name="ssq", tag="ssq%d" % a)
            st["ssq", p, a] = ssq
            junk = work.tile([P, 512], BF16, name="junk", tag="junk")
            nc.scalar.activation(out=junk[:], in_=st["c", p, a][:], func=ACT.Square, accum_out=ssq[:])

        def sr(p, a):
            rstd = work.tile([P, 1], F32, name="rstd", tag="rstd%d" % a)
            st["rstd", p, a] = rstd
            nc.scalar.activation(
                out=rstd[:],
                in_=st["ssq", p, a][:],
                func=ACT.Abs_reciprocal_sqrt,
                scale=1.0 / 512.0,
                bias=eps_t[:],
            )

        def hh(p, a):
            h = work.tile([P, 512], BF16, name="h%d" % a, tag="h%d" % a)
            st["h", p, a] = h
            nc.vector.scalar_tensor_tensor(
                out=h[:],
                in0=st["c", p, a][:],
                scalar=st["rstd", p, a][:],
                in1=w_bc[:],
                op0=ALU.mult,
                op1=ALU.mult,
            )

        def th(p):
            ht = psum.tile([P, 2, 4, P], BF16, name="ht", tag="ht")
            st["ht", p] = ht
            for a in range(2):
                for t in range(4):
                    nc.tensor.matmul(
                        out=ht[:, a, t, :], lhsT=st["h", p, a][:, t * P : (t + 1) * P], rhs=ident_b[:], start=True, stop=True
                    )

        def ch(p):
            gh = work.tile([P, 1024], BF16, name="gh", tag="gh", align_bytes=64)
            st["gh", p] = gh
            nc.scalar.copy(
                out=gh[:].rearrange("p (a r t) -> p a r t", a=2, t=4),
                in_=st["ht", p][:].rearrange("p a t r -> p a r t"),
            )

        def qh(p):
            hq = work.tile([P, 256], U32, name="hq", tag="hq", align_bytes=64)
            hs = work.tile([P, 256], U8, name="hs", tag="hs", align_bytes=64)
            st["hq", p] = (hq, hs)
            nc.vector.quantize_mx(out=hq[:].bitcast(FP8X4), scales=hs[:], in_=st["gh", p][:])

        def m2(p, a, z):
            kind = "nr"[z]
            acc = psum.tile([P, 512], F32, name="%s%d" % (kind, a), tag="%s%d" % (kind, a))
            st[kind, p, a] = acc
            hq, hs = st["hq", p]
            nc.tensor.matmul_mx(
                out=acc[:],
                lhsT=hq[:, a * P : (a + 1) * P].bitcast(FP8X4),
                lhsT_scale=hs[:, a * P : (a + 1) * P],
                rhs=wb_q[:, z * 512 : (z + 1) * 512].bitcast(FP8X4),
                rhs_scale=wb_s[:, z * 512 : (z + 1) * 512],
                start=True,
                stop=True,
            )

        def out_tile(u):
            if ("o", u) not in st:
                st["o", u] = outp.tile([P, HEADS, 4, P], F32, name="o_sb", tag="o_sb")
            return st["o", u]

        def cn(p, a):
            k = 2 * p + a
            nc.scalar.copy(
                out=out_tile(k // 4)[:, :, k % 4, 0:64],
                in_=st["n", p, a][:].rearrange("p (h f) -> p h f", h=HEADS),
            )

        def tt(p, a):
            k = 2 * p + a
            c = ((k // 4) % 2) * 4 + k % 4
            prod = work.tile([P, 2, HEADS, 64], F32, name="prod", tag="prod")
            st["t", p, a] = prod
            nc.vector.tensor_tensor(
                out=prod[:],
                in0=st["r", p, a][:].rearrange("p (h f) -> p h f", h=HEADS).unsqueeze(1).to_broadcast([P, 2, HEADS, 64]),
                in1=tab[:, c].rearrange("p z s f -> p z (s f)").unsqueeze(2).to_broadcast([P, 2, HEADS, 64]),
                op=ALU.mult,
            )

        def ad(p, a):
            k = 2 * p + a
            prod = st["t", p, a]
            engine = nc.vector if p == N_PAIRS - 1 else nc.gpsimd
            engine.tensor_tensor(
                out=out_tile(k // 4)[:, :, k % 4, 64:128].rearrange("p h (i e) -> p h i e", e=2),
                in0=prod[:, 0].rearrange("p h (i e) -> p h i e", e=2),
                in1=prod[:, 1].rearrange("p h (i e) -> p h i e", e=2)[:, :, :, ::-1],
                op=ALU.add,
            )

        def store(u, lo, hi):
            dst = out[u // 2].rearrange("h (q p i) f -> q p h (i f)", q=2, p=P, i=4)[u % 2]
            nc.sync.dma_start(
                out=dst[:, :, lo * P : hi * P],
                in_=st["o", u][:, :, lo:hi, :].rearrange("p h i f -> p h (i f)"),
            )

        def done(p, a):
            if p == N_PAIRS - 1:
                store(N_UNITS - 1, 2 + a, 3 + a)
            elif p == N_PAIRS - 2 and a == 1:
                store(N_UNITS - 1, 0, 2)
            elif p % 2 == 1 and a == 1:
                store(p // 2, 0, 4)

        def run(stage, p, *rest):
            if 0 <= p < N_PAIRS:
                stage(p, *rest)

        def x_stage(q):
            run(tx, q)
            run(cx, q - 2)
            run(qx, q - 3)
            if q == 3:
                spread_gain()

        tables()
        for n in range(-1, N_PAIRS + 4):
            x_stage(4 * n + 4)
            run(m1, n, 0)
            run(m2, n - 3, 0, 1)
            run(hh, n - 1, 1)
            run(m1, n, 1)
            run(tt, n - 3, 0)
            x_stage(4 * n + 5)
            run(ch, n - 2)
            run(sq, n, 0)
            run(ad, n - 4, 0)
            run(done, n - 4, 0)
            run(sq, n, 1)
            run(sr, n, 0)
            x_stage(4 * n + 6)
            run(m2, n - 3, 0, 0)
            run(m2, n - 3, 1, 1)
            run(cn, n - 3, 0)
            run(m2, n - 3, 1, 0)
            run(qh, n - 2)
            run(th, n - 1)
            run(sr, n, 1)
            x_stage(4 * n + 7)
            run(cn, n - 3, 1)
            run(hh, n, 0)
            run(ad, n - 4, 1)
            run(done, n - 4, 1)
            run(tt, n - 3, 1)
            if n == 0:
                wb_rope()
            if n == 1:
                wb_nope()
